import numpy as np
import ml_dtypes


def mxq(x, axis, fmt="e4m3"):
    dtype, down = {"e4m3": (ml_dtypes.float8_e4m3fn, 7), "e5m2": (ml_dtypes.float8_e5m2, 14)}[fmt]
    v = np.moveaxis(np.asarray(x, np.float32).astype(ml_dtypes.bfloat16).astype(np.float64), axis, -1)
    blocks = v.reshape(v.shape[:-1] + (-1, 32))
    amax = np.abs(blocks).max(-1, keepdims=True)
    byte = np.maximum(np.where(amax > 0, np.frexp(amax)[1] - 1 + 127, 0) - down, 1)
    scale = np.exp2(byte - 127.0)
    codes = (blocks / scale).astype(np.float32).astype(dtype).astype(np.float64)
    return np.moveaxis((codes * scale).reshape(v.shape), -1, axis)


WIDE = False


def mx_kscale(k):
    if not WIDE:
        return np.ones(k)
    levels = np.array([10, -10, 5, -5, 0])
    if k % 512:
        return np.exp2(np.random.permutation(np.resize(levels, k // 32))).repeat(32)
    a = np.empty((k // 512, 16))
    for p in range(k // 512):
        a[p, :8] = np.random.permutation(np.resize(levels, 8))
        for g in range(8):
            far = levels[np.abs(levels - a[p, g]) >= 10]
            a[p, g + 8] = far[np.random.randint(len(far))]
    return np.exp2(a.ravel()).repeat(32)


BF16 = ml_dtypes.bfloat16


def bf(x):
    return np.asarray(x, np.float32).astype(BF16)


def f64(x):
    return np.asarray(x).astype(np.float64)


B, L, E, H, DH, RK, RD, MAXLEN = 4, 128, 2048, 16, 128, 512, 128, 4096


def apply_rope(x, cos, sin):
    cos = cos[None, :, None, :]
    sin = sin[None, :, None, :]
    x1, x2 = x[..., 0::2], x[..., 1::2]
    out_real = x1 * cos - x2 * sin
    out_imag = x1 * sin + x2 * cos
    return np.stack([out_real, out_imag], axis=-1).reshape(x.shape)


def setup_inputs():
    s = mx_kscale(E)
    return {"x": bf(np.random.standard_normal((B, L, E)) * s),
            "cos": bf(np.random.uniform(size=(L, RD // 2))),
            "sin": bf(np.random.uniform(size=(L, RD // 2))),
            "wq": bf(np.random.standard_normal((E, H * (DH + RD))) / np.sqrt(E) / s[:, None])}


def core(x, cos, sin, wq):
    q_all = (mxq(f64(x), 2, "e4m3") @ mxq(f64(wq), 0, "e4m3")).reshape(B, L, H, DH + RD)
    q_head, q_rope = q_all[..., :DH], q_all[..., DH:]
    q_rope = apply_rope(q_rope, f64(cos), f64(sin))
    return np.concatenate([q_head, q_rope], axis=-1)


def e4m3fn_bytes(y):
    return np.clip(np.asarray(y, np.float64), -448.0, 448.0).astype(np.float32).astype(ml_dtypes.float8_e4m3fn).view(np.uint8)


def reference(x, cos, sin, wq):
    out = core(x, cos, sin, wq)
    s = np.max(np.abs(out), axis=-1, keepdims=True) / 448.0
    return out, e4m3fn_bytes(out / s)

@@ -1,0 +1,357 @@
+from contextlib import ExitStack
+
+import concourse.mybir as mybir
+from concourse.masks import make_identity
+
+FLOPS = 2 * 512 * 2048 * 4096
+
+F32 = mybir.dt.float32
+BF16 = mybir.dt.bfloat16
+U32 = mybir.dt.uint32
+U8 = mybir.dt.uint8
+FP8X4 = mybir.dt.float8_e4m3fn_x4
+FP8 = mybir.dt.float8_e4m3fn
+ALU = mybir.AluOpType
+ACT = mybir.ActivationFunctionType
+AX = mybir.AxisListType
+
+P = 128
+NB = 4
+NG = 4
+ROPE, CONT = 1, 0
+
+MANUAL = True
+SIZES = (4, 4, 4, 4)
+WHO = ("VVVVVVVVSSSSSSSS", "SSSSGGSSVSPPPPPP", "SSSSGGSSVSPPPPPP", "SSSSGGSSVSPPPPPP")
+PRE = 4
+CAST = ("VVVS", "VVVV", "VSSS", "VVSV")
+XCOPY = "SS"
+EVPER = 1
+SPLIT = 2
+
+
+def tile_multiheadlatentattention_pb_kernel(tc, x, cos, sin, wq, out_0, out_1):
+    nc = tc.nc
+    ngr = len(SIZES)
+    first = [sum(SIZES[0:i]) for i in range(ngr)]
+    with ExitStack() as ctx:
+        const = ctx.enter_context(tc.tile_pool(name="const", bufs=1))
+        rawp = ctx.enter_context(tc.tile_pool(name="rawp", bufs=12))
+        grp = ctx.enter_context(tc.tile_pool(name="grp", bufs=8))
+        cdp = ctx.enter_context(tc.tile_pool(name="cdp", bufs=3))
+        otp = ctx.enter_context(tc.tile_pool(name="otp", bufs=8))
+        tmp = ctx.enter_context(tc.tile_pool(name="tmp", bufs=4))
+        o8p = ctx.enter_context(tc.tile_pool(name="o8p", bufs=8))
+        smp = ctx.enter_context(tc.tile_pool(name="smp", bufs=3))
+        psum = ctx.enter_context(tc.psum_pool(name="psum", bufs=1))
+        if MANUAL:
+            ctx.enter_context(tc.manual_schedule())
+
+        zero = const.tile([P, 1], F32, name="zero")
+        nc.vector.memset(zero[:], 0.0)
+        junk = const.tile([P, 1], F32, name="junk")
+        nc.scalar.activation(out=junk[:], in_=zero[:], func=ACT.Identity, scale=zero[:, 0:1], bias=zero[:, 0:1])
+        cosb = const.tile([P, 64], BF16, name="cosb")
+        sinb = const.tile([P, 64], BF16, name="sinb")
+        nc.sync.dma_start(out=cosb[:], in_=cos)
+        nc.sync.dma_start(out=sinb[:], in_=sin)
+        ident = const.tile([P, P], F32, name="ident")
+        make_identity(nc, ident[:])
+        identb = const.tile([P, P], BF16, name="identb")
+        make_identity(nc, identb[:])
+
+        xr = {}
+        raw = {}
+
+        def load_x(b):
+            t = rawp.tile([P, 2048], BF16, name="xr%d" % b, tag="raw")
+            nc.sync.dma_start(out=t[:], in_=x[b])
+            xr[b] = t
+
+        def load_w1(gi, g):
+            c0, wd = 256 * first[gi], 256 * SIZES[gi]
+            t = rawp.tile([P, 4, wd], BF16, name="raw%d_%d" % (gi, g), tag="raw")
+            nc.sync.dma_start(
+                out=t[:],
+                in_=wq[512 * g:512 * (g + 1), c0:c0 + wd].rearrange("(p j) n -> p j n", j=4),
+            )
+            raw[(gi, g)] = t
+
+        def load_w(gi):
+            for g in range(NG):
+                load_w1(gi, g)
+
+        for b in range(NB):
+            load_x(b)
+            load_w1(0, b)
+        load_w(1)
+
+        tab = const.tile([P, 2, 512], F32, name="tab")
+        tabv = tab[:].rearrange("p t (h j e) -> p t h j e", h=4, e=2)
+        for h in range(4):
+            for e in range(2):
+                nc.vector.tensor_copy(out=tabv[:, 0, h, :, e], in_=cosb[:])
+            nc.vector.tensor_copy(out=tabv[:, 1, h, :, 0], in_=sinb[:])
+            nc.vector.tensor_scalar(out=tabv[:, 1, h, :, 1], in0=sinb[:], scalar1=-1.0, scalar2=None, op0=ALU.mult)
+
+        xc = const.tile([P, NB, 512], U32, name="xc", align_bytes=64)
+        xs = const.tile([P, NB, 512], U8, name="xs", align_bytes=64)
+        xg = {}
+
+        def x_transpose(b):
+            words = xr[b][:].bitcast(F32)
+            xg[b] = grp.tile([P, 2048], BF16, name="xg%d" % b, tag="gr", align_bytes=64)
+            xgw = xg[b][:].bitcast(F32)
+            for half in range(2):
+                pt = psum.tile([P, 512], F32, name="pt%d_%d" % (b, half), tag="%s%d" % ("rc"[half], b))
+                for gg in range(2):
+                    g = 2 * half + gg
+                    for u in range(2):
+                        nc.tensor.transpose(pt[:, (2 * gg + u) * P:(2 * gg + u + 1) * P],
+                                            words[:, 256 * g + u:256 * (g + 1):2], ident[:])
+                dst = xgw[:, 512 * half:512 * (half + 1)].rearrange("p (g r u) -> p g r u", g=2, u=2)
+                src = pt[:].rearrange("p (g u r) -> p g r u", g=2, u=2)
+                if XCOPY[half] == "V":
+                    nc.vector.tensor_copy(out=dst, in_=src)
+                else:
+                    nc.scalar.copy(out=dst, in_=src)
+
+        def x_quant(b):
+            nc.vector.quantize_mx(out=xc[:, b, :].bitcast(FP8X4), scales=xs[:, b, :], in_=xg[b][:])
+
+        grs = {}
+        wcs = {}
+        accs = {}
+        UNITS = [(ROPE, g) for g in range(NG)] + [(CONT, g) for g in range(NG)]
+        fills = [0]
+        pbs = {}
+
+        def interleave(gi, hu):
+            s, g = UNITS[hu // 2]
+            hh = hu % 2
+            hp = SIZES[gi]
+            eng = WHO[gi][hu]
+            if (gi, s, g) not in grs:
+                grs[(gi, s, g)] = grp.tile([P, 512 * hp], BF16, name="gr%d_%d_%d" % (gi, s, g), tag="gr",
+                                           align_bytes=64)
+            gr = grs[(gi, s, g)]
+            hn = hp // 2
+            src = raw[(gi, g)][:].rearrange("p j (h s d) -> p j h s d", h=hp, s=2)[:, :, hn * hh:hn * (hh + 1), s, :]
+            if eng == "P":
+                pb = psum.tile([P, 512 * hn], BF16, name="pb%d_%d" % (gi, hu), tag="c%d" % (fills[0] % NB))
+                fills[0] += 1
+                pbv = pb[:].rearrange("p (h d j) -> p h d j", h=hn, j=4)
+                for j0 in (0, 2):
+                    nc.tensor.matmul(out=pbv[:, :, :, j0:j0 + 2], lhsT=identb[:],
+                                     rhs=src[:, j0:j0 + 2, :, :].rearrange("p e h d -> p h d e"),
+                                     start=True, stop=True)
+                pbs[(gi, hu)] = pb
+                return
+            src = src.rearrange("p j h d -> p h d j")
+            dst = gr[:, 512 * hn * hh:512 * hn * (hh + 1)].rearrange("p (h d j) -> p h d j", h=hn, j=4)
+            if eng == "V":
+                nc.vector.tensor_copy(out=dst, in_=src)
+            elif eng == "S":
+                nc.scalar.copy(out=dst, in_=src)
+            else:
+                nc.gpsimd.tensor_scalar(out=dst, in0=src, scalar1=1.0, scalar2=0.0, op0=ALU.mult, op1=ALU.add)
+
+        def evac(gi, hu):
+            s, g = UNITS[hu // 2]
+            n = 256 * SIZES[gi]
+            nc.scalar.copy(out=grs[(gi, s, g)][:, n * (hu % 2):n * (hu % 2 + 1)], in_=pbs[(gi, hu)][:])
+
+        def both(gi, k, eng):
+            for hu in (2 * k, 2 * k + 1):
+                if WHO[gi][hu] == eng:
+                    interleave(gi, hu)
+
+        def quant(gi, k):
+            s, g = UNITS[k]
+            n = 128 * SIZES[gi]
+            if g == 0:
+                wc = cdp.tile([P, NG, n], U32, name="wc%d_%d" % (gi, s), tag="wc", align_bytes=64)
+                ws = cdp.tile([P, NG, n], U8, name="ws%d_%d" % (gi, s), tag="ws", align_bytes=64)
+                wcs[(gi, s)] = (wc, ws)
+            wc, ws = wcs[(gi, s)]
+            nc.vector.quantize_mx(out=wc[:, g, :].bitcast(FP8X4), scales=ws[:, g, :], in_=grs[(gi, s, g)][:])
+
+        def mm(gi, k, b):
+            s, g = UNITS[k]
+            if g == 0:
+                accs[(gi, s, b)] = psum.tile([P, 128 * SIZES[gi]], F32, name="acc%d_%d_%d" % (gi, s, b),
+                                             tag="%s%d" % ("cr"[s], b))
+            wc, ws = wcs[(gi, s)]
+            nc.tensor.matmul_mx(
+                out=accs[(gi, s, b)][:],
+                lhsT=xc[:, b, P * g:P * (g + 1)].bitcast(FP8X4),
+                lhsT_scale=xs[:, b, P * g:P * (g + 1)],
+                rhs=wc[:, g, :].bitcast(FP8X4),
+                rhs_scale=ws[:, g, :],
+                start=(g == 0),
+                stop=(g == NG - 1),
+            )
+
+        def quant_mm(gi, k):
+            quant(gi, k)
+            for b in range(NB):
+                mm(gi, k, b)
+
+        ots = {}
+        ams = {}
+
+        def rope(gi, b):
+            hp = SIZES[gi]
+            acc = accs[(gi, ROPE, b)]
+            ot = otp.tile([P, 256 * hp], F32, name="ot%d_%d" % (gi, b), tag="ot")
+            ots[(gi, b)] = ot
+            t12 = tmp.tile([P, 2, 128 * hp], F32, name="t12_%d_%d" % (gi, b), tag="t12")
+            nc.vector.tensor_tensor(out=t12[:], in0=acc[:].unsqueeze(1).to_broadcast([P, 2, 128 * hp]),
+                                    in1=tab[:, :, 0:128 * hp], op=ALU.mult)
+            nc.gpsimd.tensor_tensor(
+                out=ot[:].rearrange("p (h s j e) -> p h s j e", h=hp, s=2, e=2)[:, :, 1, :, :],
+                in0=t12[:, 0, :].rearrange("p (h j e) -> p h j e", h=hp, e=2),
+                in1=t12[:, 1, :].rearrange("p (h j e) -> p h j e", h=hp, e=2)[:, :, :, ::-1],
+                op=ALU.add,
+            )
+
+        def content(gi, b):
+            hp = SIZES[gi]
+            nc.scalar.copy(
+                out=ots[(gi, b)][:].rearrange("p (h s d) -> p h s d", h=hp, s=2)[:, :, 0, :],
+                in_=accs[(gi, CONT, b)][:].rearrange("p (h d) -> p h d", h=hp),
+            )
+            nc.sync.dma_start(out=out_0[b, :, first[gi]:first[gi] + hp, :].rearrange("l h d -> l (h d)"),
+                              in_=ots[(gi, b)][:])
+
+        def amax(gi, b):
+            hp = SIZES[gi]
+            if b == 0:
+                am = smp.tile([P, NB * hp], F32, name="am%d" % gi, tag="am")
+                rc = smp.tile([P, NB * hp], F32, name="rc%d" % gi, tag="rc")
+                rs = smp.tile([P, NB * hp], F32, name="rs%d" % gi, tag="rs")
+                ams[gi] = (am, rc, rs)
+            am = ams[gi][0]
+            nc.vector.tensor_reduce(out=am[:, hp * b:hp * (b + 1)],
+                                    in_=ots[(gi, b)][:].rearrange("p (h c) -> p h c", h=hp), axis=AX.X,
+                                    op=ALU.max, apply_absolute_value=True)
+
+        def recip(gi):
+            am, rc, rs = ams[gi]
+            nc.vector.reciprocal(out=rc[:], in_=am[:])
+
+        def factor(gi):
+            am, rc, rs = ams[gi]
+            nc.vector.tensor_scalar(out=rs[:], in0=rc[:], scalar1=448.0, scalar2=None, op0=ALU.mult)
+
+        o8s = {}
+
+        def casts(gi, b, eng):
+            hp = SIZES[gi]
+            rs = ams[gi][2]
+            ot = ots[(gi, b)]
+            if (gi, b) not in o8s:
+                o8s[(gi, b)] = o8p.tile([P, 256 * hp], FP8, name="o8_%d_%d" % (gi, b), tag="o8")
+            o8 = o8s[(gi, b)]
+            for h in range(hp):
+                cols = slice(256 * h, 256 * (h + 1))
+                fac = rs[:, hp * b + h:hp * b + h + 1]
+                if CAST[gi][h] != eng:
+                    continue
+                if eng == "V":
+                    nc.vector.tensor_scalar(out=o8[:, cols], in0=ot[:, cols], scalar1=fac, scalar2=None,
+                                            op0=ALU.mult, saturate=False)
+                else:
+                    nc.scalar.activation(out=o8[:, cols], in_=ot[:, cols], func=ACT.Identity,
+                                         scale=fac, bias=zero[:, 0:1], saturate=False)
+
+        def store8(gi, b):
+            hp = SIZES[gi]
+            nc.sync.dma_start(out=out_1[b, :, first[gi]:first[gi] + hp, :].rearrange("l h d -> l (h d)"),
+                              in_=o8s[(gi, b)][:].bitcast(U8))
+
+        def s_list(gi):
+            return [hu for hu in range(16) if WHO[gi][hu] == "S"]
+
+        x_transpose(0)
+        for t in range(NB):
+            for k in (t, 4 + t):
+                both(0, k, "V")
+                both(0, k, "S")
+            x_quant(t)
+            if t + 1 < NB:
+                x_transpose(t + 1)
+            else:
+                for hu in s_list(1)[0:PRE]:
+                    interleave(1, hu)
+            quant(0, t)
+            quant(0, 4 + t)
+            for part in (0, 4):
+                for b in range(t):
+                    mm(0, part + t, b)
+                for g in range(t + 1):
+                    mm(0, part + g, t)
+
+        for gi in range(ngr):
+            nxt = gi + 1
+            if gi + 2 < ngr:
+                load_w(gi + 2)
+            last = nxt >= ngr
+            for b in range(NB):
+                rope(gi, b)
+            if gi > 0:
+                for b in range(SPLIT):
+                    casts(gi - 1, b, "S")
+                    store8(gi - 1, b)
+            for b in range(NB):
+                content(gi, b)
+            others = []
+            if gi > 0:
+                for b in range(SPLIT, NB):
+                    others.append(("cast", b))
+            plist = []
+            if not last:
+                for hu in range(16):
+                    if WHO[nxt][hu] == "G":
+                        interleave(nxt, hu)
+                plist = [hu for hu in range(16) if WHO[nxt][hu] == "P"]
+                for hu in s_list(nxt)[PRE:]:
+                    others.append(("il", hu))
+                for hu in plist[0:NB]:
+                    interleave(nxt, hu)
+            nev = 0
+            while others or nev < len(plist):
+                if others:
+                    what, arg = others.pop(0)
+                    if what == "cast":
+                        casts(gi - 1, arg, "S")
+                        store8(gi - 1, arg)
+                    else:
+                        interleave(nxt, arg)
+                for rep in range(EVPER):
+                    if nev < len(plist):
+                        evac(nxt, plist[nev])
+                        if nev + NB < len(plist):
+                            interleave(nxt, plist[nev + NB])
+                        nev += 1
+            for b in range(NB):
+                amax(gi, b)
+            recip(gi)
+            if last:
+                factor(gi)
+                for b in range(NB):
+                    casts(gi, b, "V")
+                    casts(gi, b, "S")
+                    store8(gi, b)
+            else:
+                both(nxt, 0, "V")
+                quant_mm(nxt, 0)
+                factor(gi)
+                for k in range(1, 8):
+                    both(nxt, k, "V")
+                    if k <= NB:
+                        casts(gi, k - 1, "V")
+                    quant_mm(nxt, k)
+                if nxt + 1 < ngr:
+                    for hu in s_list(nxt + 1)[0:PRE]:
+                        interleave(nxt + 1, hu)

@@ -27,6 +27,8 @@ PRE = 4
 CAST = ("VVVS", "VVVV", "VSSS", "VVSV")
 XCOPY = "SS"
 EVPER = 1
+RUN = 4
+RUNS = "VS"
 SPLIT = 2
 
 
@@ -147,8 +149,12 @@ def tile_multiheadlatentattention_pb_kernel(tc, x, cos, sin, wq, out_0, out_1):
                                      start=True, stop=True)
                 pbs[(gi, hu)] = pb
                 return
-            src = src.rearrange("p j h d -> p h d j")
-            dst = gr[:, 512 * hn * hh:512 * hn * (hh + 1)].rearrange("p (h d j) -> p h d j", h=hn, j=4)
+            if eng in RUNS:
+                src = src.rearrange("p j h (c i) -> p h c j i", i=RUN)
+                dst = gr[:, 512 * hn * hh:512 * hn * (hh + 1)].rearrange("p (h c i j) -> p h c j i", h=hn, i=RUN, j=4)
+            else:
+                src = src.rearrange("p j h d -> p h d j")
+                dst = gr[:, 512 * hn * hh:512 * hn * (hh + 1)].rearrange("p (h d j) -> p h d j", h=hn, j=4)
             if eng == "V":
                 nc.vector.tensor_copy(out=dst, in_=src)
             elif eng == "S":

@@ -24,7 +24,7 @@ MANUAL = True
 SIZES = (4, 4, 4, 4)
 WHO = ("VVVVVVVVSSSSSSSS", "SSSSGGSSVSPPPPPP", "SSSSGGSSVSPPPPPP", "SSSSGGSSVSPPPPPP")
 PRE = 4
-CAST = ("VVVS", "VVVV", "VSSS", "VVSV")
+CAST = ("VVVS", "VSSS", "SSSS", "VVSV")
 XCOPY = "SS"
 EVPER = 1
 RUN = 4
@@ -312,9 +312,6 @@ def tile_multiheadlatentattention_pb_kernel(tc, x, cos, sin, wq, out_0, out_1):
             for b in range(NB):
                 content(gi, b)
             others = []
-            if gi > 0:
-                for b in range(SPLIT, NB):
-                    others.append(("cast", b))
             plist = []
             if not last:
                 for hu in range(16):
@@ -325,6 +322,9 @@ def tile_multiheadlatentattention_pb_kernel(tc, x, cos, sin, wq, out_0, out_1):
                     others.append(("il", hu))
                 for hu in plist[0:NB]:
                     interleave(nxt, hu)
+            if gi > 0:
+                for b in range(SPLIT, NB):
+                    others.append(("cast", b))
             nev = 0
             while others or nev < len(plist):
                 if others:

@@ -144,8 +144,8 @@ def tile_multiheadlatentattention_pb_kernel(tc, x, cos, sin, wq, out_0, out_1):
                 fills[0] += 1
                 pbv = pb[:].rearrange("p (h d j) -> p h d j", h=hn, j=4)
                 for j0 in (0, 2):
-                    nc.tensor.matmul(out=pbv[:, :, :, j0:j0 + 2], lhsT=identb[:],
-                                     rhs=src[:, j0:j0 + 2, :, :].rearrange("p e h d -> p h d e"),
+                    nc.tensor.matmul(out=pbv[:, :, :, j0:j0 + 2].rearrange("p h d e -> p e h d"), lhsT=identb[:],
+                                     rhs=src[:, j0:j0 + 2, :, :],
                                      start=True, stop=True)
                 pbs[(gi, hu)] = pb
                 return

from contextlib import ExitStack

import concourse.mybir as mybir
from concourse.masks import make_identity

FLOPS = 2 * 512 * 2048 * 4096

F32 = mybir.dt.float32
BF16 = mybir.dt.bfloat16
U32 = mybir.dt.uint32
U8 = mybir.dt.uint8
FP8X4 = mybir.dt.float8_e4m3fn_x4
FP8 = mybir.dt.float8_e4m3fn
ALU = mybir.AluOpType
ACT = mybir.ActivationFunctionType
AX = mybir.AxisListType

P = 128
NB = 4
NG = 4
ROPE, CONT = 1, 0

MANUAL = True
SIZES = (4, 4, 4, 4)
WHO = ("VVVVVVVVSSSSSSSS", "SSSSGGSSVSPPPPPP", "SSSSGGSSVSPPPPPP", "SSSSGGSSVSPPPPPP")
PRE = 4
CAST = ("VVVS", "VSSS", "SSSS", "VVSV")
XCOPY = "SS"
EVPER = 1
RUN = 4
RUNS = "VS"
SPLIT = 2


def tile_multiheadlatentattention_pb_kernel(tc, x, cos, sin, wq, out_0, out_1):
    nc = tc.nc
    ngr = len(SIZES)
    first = [sum(SIZES[0:i]) for i in range(ngr)]
    with ExitStack() as ctx:
        const = ctx.enter_context(tc.tile_pool(name="const", bufs=1))
        rawp = ctx.enter_context(tc.tile_pool(name="rawp", bufs=12))
        grp = ctx.enter_context(tc.tile_pool(name="grp", bufs=8))
        cdp = ctx.enter_context(tc.tile_pool(name="cdp", bufs=3))
        otp = ctx.enter_context(tc.tile_pool(name="otp", bufs=8))
        tmp = ctx.enter_context(tc.tile_pool(name="tmp", bufs=4))
        o8p = ctx.enter_context(tc.tile_pool(name="o8p", bufs=8))
        smp = ctx.enter_context(tc.tile_pool(name="smp", bufs=3))
        psum = ctx.enter_context(tc.psum_pool(name="psum", bufs=1))
        if MANUAL:
            ctx.enter_context(tc.manual_schedule())

        zero = const.tile([P, 1], F32, name="zero")
        nc.vector.memset(zero[:], 0.0)
        junk = const.tile([P, 1], F32, name="junk")
        nc.scalar.activation(out=junk[:], in_=zero[:], func=ACT.Identity, scale=zero[:, 0:1], bias=zero[:, 0:1])
        cosb = const.tile([P, 64], BF16, name="cosb")
        sinb = const.tile([P, 64], BF16, name="sinb")
        nc.sync.dma_start(out=cosb[:], in_=cos)
        nc.sync.dma_start(out=sinb[:], in_=sin)
        ident = const.tile([P, P], F32, name="ident")
        make_identity(nc, ident[:])
        identb = const.tile([P, P], BF16, name="identb")
        make_identity(nc, identb[:])

        xr = {}
        raw = {}

        def load_x(b):
            t = rawp.tile([P, 2048], BF16, name="xr%d" % b, tag="raw")
            nc.sync.dma_start(out=t[:], in_=x[b])
            xr[b] = t

        def load_w1(gi, g):
            c0, wd = 256 * first[gi], 256 * SIZES[gi]
            t = rawp.tile([P, 4, wd], BF16, name="raw%d_%d" % (gi, g), tag="raw")
            nc.sync.dma_start(
                out=t[:],
                in_=wq[512 * g:512 * (g + 1), c0:c0 + wd].rearrange("(p j) n -> p j n", j=4),
            )
            raw[(gi, g)] = t

        def load_w(gi):
            for g in range(NG):
                load_w1(gi, g)

        for b in range(NB):
            load_x(b)
            load_w1(0, b)
        load_w(1)

        tab = const.tile([P, 2, 512], F32, name="tab")
        tabv = tab[:].rearrange("p t (h j e) -> p t h j e", h=4, e=2)
        for h in range(4):
            for e in range(2):
                nc.vector.tensor_copy(out=tabv[:, 0, h, :, e], in_=cosb[:])
            nc.vector.tensor_copy(out=tabv[:, 1, h, :, 0], in_=sinb[:])
            nc.vector.tensor_scalar(out=tabv[:, 1, h, :, 1], in0=sinb[:], scalar1=-1.0, scalar2=None, op0=ALU.mult)

        xc = const.tile([P, NB, 512], U32, name="xc", align_bytes=64)
        xs = const.tile([P, NB, 512], U8, name="xs", align_bytes=64)
        xg = {}

        def x_transpose(b):
            words = xr[b][:].bitcast(F32)
            xg[b] = grp.tile([P, 2048], BF16, name="xg%d" % b, tag="gr", align_bytes=64)
            xgw = xg[b][:].bitcast(F32)
            for half in range(2):
                pt = psum.tile([P, 512], F32, name="pt%d_%d" % (b, half), tag="%s%d" % ("rc"[half], b))
                for gg in range(2):
                    g = 2 * half + gg
                    for u in range(2):
                        nc.tensor.transpose(pt[:, (2 * gg + u) * P:(2 * gg + u + 1) * P],
                                            words[:, 256 * g + u:256 * (g + 1):2], ident[:])
                dst = xgw[:, 512 * half:512 * (half + 1)].rearrange("p (g r u) -> p g r u", g=2, u=2)
                src = pt[:].rearrange("p (g u r) -> p g r u", g=2, u=2)
                if XCOPY[half] == "V":
                    nc.vector.tensor_copy(out=dst, in_=src)
                else:
                    nc.scalar.copy(out=dst, in_=src)

        def x_quant(b):
            nc.vector.quantize_mx(out=xc[:, b, :].bitcast(FP8X4), scales=xs[:, b, :], in_=xg[b][:])

        grs = {}
        wcs = {}
        accs = {}
        UNITS = [(ROPE, g) for g in range(NG)] + [(CONT, g) for g in range(NG)]
        fills = [0]
        pbs = {}

        def interleave(gi, hu):
            s, g = UNITS[hu // 2]
            hh = hu % 2
            hp = SIZES[gi]
            eng = WHO[gi][hu]
            if (gi, s, g) not in grs:
                grs[(gi, s, g)] = grp.tile([P, 512 * hp], BF16, name="gr%d_%d_%d" % (gi, s, g), tag="gr",
                                           align_bytes=64)
            gr = grs[(gi, s, g)]
            hn = hp // 2
            src = raw[(gi, g)][:].rearrange("p j (h s d) -> p j h s d", h=hp, s=2)[:, :, hn * hh:hn * (hh + 1), s, :]
            if eng == "P":
                pb = psum.tile([P, 512 * hn], BF16, name="pb%d_%d" % (gi, hu), tag="c%d" % (fills[0] % NB))
                fills[0] += 1
                pbv = pb[:].rearrange("p (h d j) -> p h d j", h=hn, j=4)
                for j0 in (0, 2):
                    nc.tensor.matmul(out=pbv[:, :, :, j0:j0 + 2].rearrange("p h d e -> p e h d"), lhsT=identb[:],
                                     rhs=src[:, j0:j0 + 2, :, :],
                                     start=True, stop=True)
                pbs[(gi, hu)] = pb
                return
            if eng in RUNS:
                src = src.rearrange("p j h (c i) -> p h c j i", i=RUN)
                dst = gr[:, 512 * hn * hh:512 * hn * (hh + 1)].rearrange("p (h c i j) -> p h c j i", h=hn, i=RUN, j=4)
            else:
                src = src.rearrange("p j h d -> p h d j")
                dst = gr[:, 512 * hn * hh:512 * hn * (hh + 1)].rearrange("p (h d j) -> p h d j", h=hn, j=4)
            if eng == "V":
                nc.vector.tensor_copy(out=dst, in_=src)
            elif eng == "S":
                nc.scalar.copy(out=dst, in_=src)
            else:
                nc.gpsimd.tensor_scalar(out=dst, in0=src, scalar1=1.0, scalar2=0.0, op0=ALU.mult, op1=ALU.add)

        def evac(gi, hu):
            s, g = UNITS[hu // 2]
            n = 256 * SIZES[gi]
            nc.scalar.copy(out=grs[(gi, s, g)][:, n * (hu % 2):n * (hu % 2 + 1)], in_=pbs[(gi, hu)][:])

        def both(gi, k, eng):
            for hu in (2 * k, 2 * k + 1):
                if WHO[gi][hu] == eng:
                    interleave(gi, hu)

        def quant(gi, k):
            s, g = UNITS[k]
            n = 128 * SIZES[gi]
            if g == 0:
                wc = cdp.tile([P, NG, n], U32, name="wc%d_%d" % (gi, s), tag="wc", align_bytes=64)
                ws = cdp.tile([P, NG, n], U8, name="ws%d_%d" % (gi, s), tag="ws", align_bytes=64)
                wcs[(gi, s)] = (wc, ws)
            wc, ws = wcs[(gi, s)]
            nc.vector.quantize_mx(out=wc[:, g, :].bitcast(FP8X4), scales=ws[:, g, :], in_=grs[(gi, s, g)][:])

        def mm(gi, k, b):
            s, g = UNITS[k]
            if g == 0:
                accs[(gi, s, b)] = psum.tile([P, 128 * SIZES[gi]], F32, name="acc%d_%d_%d" % (gi, s, b),
                                             tag="%s%d" % ("cr"[s], b))
            wc, ws = wcs[(gi, s)]
            nc.tensor.matmul_mx(
                out=accs[(gi, s, b)][:],
                lhsT=xc[:, b, P * g:P * (g + 1)].bitcast(FP8X4),
                lhsT_scale=xs[:, b, P * g:P * (g + 1)],
                rhs=wc[:, g, :].bitcast(FP8X4),
                rhs_scale=ws[:, g, :],
                start=(g == 0),
                stop=(g == NG - 1),
            )

        def quant_mm(gi, k):
            quant(gi, k)
            for b in range(NB):
                mm(gi, k, b)

        ots = {}
        ams = {}

        def rope(gi, b):
            hp = SIZES[gi]
            acc = accs[(gi, ROPE, b)]
            ot = otp.tile([P, 256 * hp], F32, name="ot%d_%d" % (gi, b), tag="ot")
            ots[(gi, b)] = ot
            t12 = tmp.tile([P, 2, 128 * hp], F32, name="t12_%d_%d" % (gi, b), tag="t12")
            nc.vector.tensor_tensor(out=t12[:], in0=acc[:].unsqueeze(1).to_broadcast([P, 2, 128 * hp]),
                                    in1=tab[:, :, 0:128 * hp], op=ALU.mult)
            nc.gpsimd.tensor_tensor(
                out=ot[:].rearrange("p (h s j e) -> p h s j e", h=hp, s=2, e=2)[:, :, 1, :, :],
                in0=t12[:, 0, :].rearrange("p (h j e) -> p h j e", h=hp, e=2),
                in1=t12[:, 1, :].rearrange("p (h j e) -> p h j e", h=hp, e=2)[:, :, :, ::-1],
                op=ALU.add,
            )

        def content(gi, b):
            hp = SIZES[gi]
            nc.scalar.copy(
                out=ots[(gi, b)][:].rearrange("p (h s d) -> p h s d", h=hp, s=2)[:, :, 0, :],
                in_=accs[(gi, CONT, b)][:].rearrange("p (h d) -> p h d", h=hp),
            )
            nc.sync.dma_start(out=out_0[b, :, first[gi]:first[gi] + hp, :].rearrange("l h d -> l (h d)"),
                              in_=ots[(gi, b)][:])

        def amax(gi, b):
            hp = SIZES[gi]
            if b == 0:
                am = smp.tile([P, NB * hp], F32, name="am%d" % gi, tag="am")
                rc = smp.tile([P, NB * hp], F32, name="rc%d" % gi, tag="rc")
                rs = smp.tile([P, NB * hp], F32, name="rs%d" % gi, tag="rs")
                ams[gi] = (am, rc, rs)
            am = ams[gi][0]
            nc.vector.tensor_reduce(out=am[:, hp * b:hp * (b + 1)],
                                    in_=ots[(gi, b)][:].rearrange("p (h c) -> p h c", h=hp), axis=AX.X,
                                    op=ALU.max, apply_absolute_value=True)

        def recip(gi):
            am, rc, rs = ams[gi]
            nc.vector.reciprocal(out=rc[:], in_=am[:])

        def factor(gi):
            am, rc, rs = ams[gi]
            nc.vector.tensor_scalar(out=rs[:], in0=rc[:], scalar1=448.0, scalar2=None, op0=ALU.mult)

        o8s = {}

        def casts(gi, b, eng):
            hp = SIZES[gi]
            rs = ams[gi][2]
            ot = ots[(gi, b)]
            if (gi, b) not in o8s:
                o8s[(gi, b)] = o8p.tile([P, 256 * hp], FP8, name="o8_%d_%d" % (gi, b), tag="o8")
            o8 = o8s[(gi, b)]
            for h in range(hp):
                cols = slice(256 * h, 256 * (h + 1))
                fac = rs[:, hp * b + h:hp * b + h + 1]
                if CAST[gi][h] != eng:
                    continue
                if eng == "V":
                    nc.vector.tensor_scalar(out=o8[:, cols], in0=ot[:, cols], scalar1=fac, scalar2=None,
                                            op0=ALU.mult, saturate=False)
                else:
                    nc.scalar.activation(out=o8[:, cols], in_=ot[:, cols], func=ACT.Identity,
                                         scale=fac, bias=zero[:, 0:1], saturate=False)

        def store8(gi, b):
            hp = SIZES[gi]
            nc.sync.dma_start(out=out_1[b, :, first[gi]:first[gi] + hp, :].rearrange("l h d -> l (h d)"),
                              in_=o8s[(gi, b)][:].bitcast(U8))

        def s_list(gi):
            return [hu for hu in range(16) if WHO[gi][hu] == "S"]

        x_transpose(0)
        for t in range(NB):
            for k in (t, 4 + t):
                both(0, k, "V")
                both(0, k, "S")
            x_quant(t)
            if t + 1 < NB:
                x_transpose(t + 1)
            else:
                for hu in s_list(1)[0:PRE]:
                    interleave(1, hu)
            quant(0, t)
            quant(0, 4 + t)
            for part in (0, 4):
                for b in range(t):
                    mm(0, part + t, b)
                for g in range(t + 1):
                    mm(0, part + g, t)

        for gi in range(ngr):
            nxt = gi + 1
            if gi + 2 < ngr:
                load_w(gi + 2)
            last = nxt >= ngr
            for b in range(NB):
                rope(gi, b)
            if gi > 0:
                for b in range(SPLIT):
                    casts(gi - 1, b, "S")
                    store8(gi - 1, b)
            for b in range(NB):
                content(gi, b)
            others = []
            plist = []
            if not last:
                for hu in range(16):
                    if WHO[nxt][hu] == "G":
                        interleave(nxt, hu)
                plist = [hu for hu in range(16) if WHO[nxt][hu] == "P"]
                for hu in s_list(nxt)[PRE:]:
                    others.append(("il", hu))
                for hu in plist[0:NB]:
                    interleave(nxt, hu)
            if gi > 0:
                for b in range(SPLIT, NB):
                    others.append(("cast", b))
            nev = 0
            while others or nev < len(plist):
                if others:
                    what, arg = others.pop(0)
                    if what == "cast":
                        casts(gi - 1, arg, "S")
                        store8(gi - 1, arg)
                    else:
                        interleave(nxt, arg)
                for rep in range(EVPER):
                    if nev < len(plist):
                        evac(nxt, plist[nev])
                        if nev + NB < len(plist):
                            interleave(nxt, plist[nev + NB])
                        nev += 1
            for b in range(NB):
                amax(gi, b)
            recip(gi)
            if last:
                factor(gi)
                for b in range(NB):
                    casts(gi, b, "V")
                    casts(gi, b, "S")
                    store8(gi, b)
            else:
                both(nxt, 0, "V")
                quant_mm(nxt, 0)
                factor(gi)
                for k in range(1, 8):
                    both(nxt, k, "V")
                    if k <= NB:
                        casts(gi, k - 1, "V")
                    quant_mm(nxt, k)
                if nxt + 1 < ngr:
                    for hu in s_list(nxt + 1)[0:PRE]:
                        interleave(nxt + 1, hu)
